import numpy as np
import ml_dtypes


def mxq(x, axis, fmt="e4m3"):
    dtype, down = {"e4m3": (ml_dtypes.float8_e4m3fn, 7), "e5m2": (ml_dtypes.float8_e5m2, 14)}[fmt]
    v = np.moveaxis(np.asarray(x, np.float32).astype(ml_dtypes.bfloat16).astype(np.float64), axis, -1)
    blocks = v.reshape(v.shape[:-1] + (-1, 32))
    amax = np.abs(blocks).max(-1, keepdims=True)
    byte = np.maximum(np.where(amax > 0, np.frexp(amax)[1] - 1 + 127, 0) - down, 1)
    scale = np.exp2(byte - 127.0)
    codes = (blocks / scale).astype(np.float32).astype(dtype).astype(np.float64)
    return np.moveaxis((codes * scale).reshape(v.shape), -1, axis)


WIDE = False


def mx_kscale(k):
    if not WIDE:
        return np.ones(k)
    levels = np.array([10, -10, 5, -5, 0])
    a = np.random.permutation(np.resize(levels, k // 512 * 4)).reshape(k // 512, 4)
    idx = np.arange(k)
    return np.exp2(a[idx // 512, idx % 128 // 32])


BF16 = ml_dtypes.bfloat16


def bf(x):
    return np.asarray(x, np.float32).astype(BF16)


def f64(x):
    return np.asarray(x).astype(np.float64)


P, N, Z, H1, H2, C = 8, 256, 16, 512, 2048, 256
EPS = 1e-5


def batch_norm(h, gamma, beta):
    mu = h.mean(axis=1, keepdims=True)
    var = h.var(axis=1, keepdims=True)
    return (h - mu) * (1.0 / np.sqrt(var + EPS)) * gamma[:, None, :] + beta[:, None, :]


def setup_inputs():
    r = np.random.standard_normal
    t = mx_kscale(H1)
    sd = np.where(np.random.random((P, 1, H1)) < 0.25, np.sqrt(EPS), 1.0)
    return {"h6_pre": bf((r((P, N, H1)) + 0.5 * r((P, 1, H1))) * sd),
            "g6": bf((1.0 + 0.1 * r((P, H1))) * t),
            "be6": bf(0.3 * r((P, H1)) * t),
            "W7": bf(r((P, H2, H1)) / np.sqrt(H1) / t),
            "b7": bf(0.3 * r((P, H2)))}


def reference(h6_pre, g6, be6, W7, b7):
    a = np.maximum(batch_norm(f64(h6_pre), f64(g6), f64(be6)), 0.0)
    y = mxq(a, 2, "e4m3") @ mxq(f64(W7), 2, "e4m3").transpose(0, 2, 1)
    return y + f64(b7)[:, None, :]

@@ -1,0 +1,241 @@
+from contextlib import ExitStack
+
+import concourse.mybir as mybir
+from concourse.masks import make_identity
+
+F32 = mybir.dt.float32
+BF16 = mybir.dt.bfloat16
+U32 = mybir.dt.uint32
+U8 = mybir.dt.uint8
+FP8X4 = mybir.dt.float8_e4m3fn_x4
+ACT = mybir.ActivationFunctionType
+ALU = mybir.AluOpType
+
+NB, N, K, J = 8, 256, 512, 2048
+EPS = 1e-5
+P = 128
+FLOPS = 2 * NB * N * K * J
+UNITS = 2 * NB
+MANUAL = False
+WBUFS = 8
+
+
+def tile_decoder_pa_kernel(tc, h6_pre, g6, be6, W7, b7, out):
+    nc = tc.nc
+    with ExitStack() as ctx:
+        const = ctx.enter_context(tc.tile_pool(name="const", bufs=1))
+        wpool = ctx.enter_context(tc.tile_pool(name="wload", bufs=WBUFS))
+        gpool = ctx.enter_context(tc.tile_pool(name="grouped", bufs=3))
+        cpool = ctx.enter_context(tc.tile_pool(name="codes", bufs=3))
+        apool = ctx.enter_context(tc.tile_pool(name="acts", bufs=2))
+        bpool = ctx.enter_context(tc.tile_pool(name="bias", bufs=3))
+        opool = ctx.enter_context(tc.tile_pool(name="outs", bufs=4))
+        tp = ctx.enter_context(tc.psum_pool(name="tp", bufs=4))
+        pp = ctx.enter_context(tc.psum_pool(name="pp", bufs=4))
+        if MANUAL:
+            ctx.enter_context(tc.manual_schedule())
+
+        ident = const.tile([P, P], F32, name="ident")
+        make_identity(nc, ident[:])
+        mhalf = const.tile([P, 4], F32, name="mhalf")
+        nc.gpsimd.memset(mhalf[:], -0.5)
+        rows = const.tile([P, 2 * P], BF16, name="rows")
+        nc.vector.memset(rows[96:128, :], 0.0)
+        nc.sync.dma_start(out=rows[0:16, :], in_=g6.rearrange("b (u w) -> (b u) w", u=2))
+        nc.sync.dma_start(out=rows[16:32, :], in_=be6.rearrange("b (u w) -> (b u) w", u=2))
+        nc.sync.dma_start(out=rows[32:96, :], in_=b7.rearrange("b (c w) -> (b c) w", c=8))
+
+        hs = const.tile([P, NB * 1024], BF16, name="hs")
+        hf = hs[:].bitcast(F32)
+
+        def load_h(b0, b1):
+            nc.sync.dma_start(
+                out=hs[:, b0 * 1024 : b1 * 1024].rearrange("p (b l k) -> p b l k", l=2, k=K),
+                in_=h6_pre[b0:b1].rearrange("b (m l) k -> m b l k", l=2),
+            )
+
+        wtiles = {}
+
+        def load_w(i):
+            b, hb = divmod(i, 2)
+            wt = wpool.tile([P, 4096], BF16, name="wsb")
+            nc.sync.dma_start(
+                out=wt[:].rearrange("p (q a k) -> p q a k", q=2, a=4),
+                in_=W7[b].rearrange("(q p a) k -> p q a k", q=4, p=P)[:, 2 * hb : 2 * hb + 2],
+            )
+            wtiles[i] = wt
+
+        load_h(0, 1)
+        load_w(0)
+        load_h(1, 2)
+        load_w(1)
+        load_h(2, NB)
+        for i in range(2, WBUFS):
+            load_w(i)
+
+        ct = tp.tile([P, 512], F32, name="ct", tag="tp")
+        nc.tensor.transpose(out=ct[:, 0:P], in_=rows[:].bitcast(F32), identity=ident[:])
+        cols = const.tile([P, P], F32, name="cols")
+        nc.scalar.copy(out=cols[:], in_=ct[:, 0:P])
+        colsb = cols[:].bitcast(BF16)
+
+        st = const.tile([P, NB * 12], F32, name="st")
+        stv = st[:].rearrange("p (i c) -> p i c", c=3)
+        vv = const.tile([P, NB * 4], F32, name="vv")
+        rr = const.tile([P, NB * 4], F32, name="rr")
+        sc = const.tile([P, NB * 4], F32, name="sc")
+        ms = const.tile([P, NB * 4], F32, name="ms")
+        sh = const.tile([P, NB * 4], F32, name="sh")
+        hts = {}
+        ats = {}
+        ags = {}
+        acs = {}
+
+        def h_stage(b):
+            ht = tp.tile([P, 512], F32, name="ht", tag="tp")
+            for u in range(2):
+                for l in range(2):
+                    src = b * 512 + l * 256 + u * P
+                    nc.tensor.transpose(
+                        out=ht[:, (u * 2 + l) * P : (u * 2 + l + 1) * P],
+                        in_=hf[:, src : src + P],
+                        identity=ident[:],
+                    )
+            hT = const.tile([P, 512], F32, name="hT%d" % b)
+            nc.scalar.copy(out=hT[:], in_=ht[:])
+            hb16 = hT[:].bitcast(BF16)
+            hts[b] = hb16
+            for u in range(2):
+                nc.vector.bn_stats(
+                    out=st[:, (b * 2 + u) * 6 : (b * 2 + u + 1) * 6],
+                    in_=hb16[:, u * 512 : (u + 1) * 512],
+                )
+            i0, i1 = 4 * b, 4 * b + 4
+            nc.gpsimd.tensor_scalar(
+                out=vv[:, i0:i1], in0=stv[:, i0:i1, 2], scalar1=1.0 / N, scalar2=EPS,
+                op0=ALU.mult, op1=ALU.add,
+            )
+            nc.gpsimd.tensor_tensor(out=rr[:, i0:i1], in0=vv[:, i0:i1], in1=mhalf[:], op=ALU.pow)
+            nc.gpsimd.tensor_tensor(out=sc[:, i0:i1], in0=rr[:, i0:i1], in1=colsb[:, i0:i1], op=ALU.mult)
+            nc.gpsimd.tensor_tensor(out=ms[:, i0:i1], in0=stv[:, i0:i1, 1], in1=sc[:, i0:i1], op=ALU.mult)
+            nc.gpsimd.tensor_tensor(
+                out=sh[:, i0:i1], in0=colsb[:, 32 + i0 : 32 + i1], in1=ms[:, i0:i1], op=ALU.subtract
+            )
+
+        def a_act(b):
+            at = apool.tile([P, 1024], BF16, name="at")
+            for u in range(2):
+                pairs = hts[b][:, u * 512 : (u + 1) * 512].rearrange("p (n e) -> p n e", e=2)
+                for e in range(2):
+                    t = 2 * u + e
+                    nc.scalar.activation(
+                        out=at[:, t * N : (t + 1) * N], in_=pairs[:, :, e], func=ACT.Relu,
+                        scale=sc[:, 4 * b + t : 4 * b + t + 1], bias=sh[:, 4 * b + t : 4 * b + t + 1],
+                    )
+            ats[b] = at
+
+        def a_regroup(b):
+            ag = apool.tile([P, 1024], BF16, name="ag", align_bytes=64)
+            nc.vector.tensor_copy(
+                out=ag[:].rearrange("p (c i t) -> p c t i", i=4, t=4),
+                in_=ats[b][:].rearrange("p (t c i) -> p c t i", t=4, i=4),
+            )
+            ags[b] = ag
+
+        def a_quant(b):
+            ac = const.tile([P, N], U32, name="ac%d" % b, align_bytes=64)
+            asc = const.tile([P, N], U8, name="as%d" % b, align_bytes=64)
+            nc.vector.quantize_mx(out=ac[:].bitcast(FP8X4), scales=asc[:], in_=ags[b][:])
+            acs[b] = (ac, asc)
+
+        bbs = {}
+        wcs = {}
+
+        def wt_stage(i):
+            b, hb = divmod(i, 2)
+            bt = tp.tile([P, 512], F32, name="bt", tag="tp")
+            for s in range(4):
+                c = 32 + b * 8 + hb * 4 + s
+                nc.tensor.transpose(
+                    out=bt[:, s * P : (s + 1) * P],
+                    in_=cols[:, c : c + 1].to_broadcast([P, P]),
+                    identity=ident[:],
+                )
+            bb = bpool.tile([P, 512], F32, name="bb")
+            nc.scalar.copy(out=bb[:], in_=bt[:])
+            bbs[i] = bb[:].bitcast(BF16)
+
+            wf = wtiles[i][:].bitcast(F32)
+            gw = gpool.tile([P, 4096], BF16, name="gw", align_bytes=64)
+            gwf = gw[:].bitcast(F32)
+            for q in range(2):
+                for ap in range(2):
+                    wt = tp.tile([P, 512], F32, name="wt", tag="tp")
+                    for al in range(2):
+                        for u in range(2):
+                            src = (q * 4 + 2 * ap + al) * 256 + u * P
+                            nc.tensor.transpose(
+                                out=wt[:, (al * 2 + u) * P : (al * 2 + u + 1) * P],
+                                in_=wf[:, src : src + P],
+                                identity=ident[:],
+                            )
+                    base = (q * 512 + ap * 256) * 2
+                    nc.scalar.copy(
+                        out=gwf[:, base : base + 512].rearrange("p (a c u) -> p a c u", a=2, u=2),
+                        in_=wt[:].rearrange("p (a u c) -> p a c u", a=2, u=2),
+                    )
+            wc = cpool.tile([P, 1024], U32, name="wc", align_bytes=64)
+            ws = cpool.tile([P, 1024], U8, name="ws", align_bytes=64)
+            nc.vector.quantize_mx(out=wc[:].bitcast(FP8X4), scales=ws[:], in_=gw[:])
+            wcs[i] = (wc, ws)
+
+        def mm_stage(i):
+            b, hb = divmod(i, 2)
+            ac, asc = acs[b]
+            wc, ws = wcs[i]
+            ot = opool.tile([P, 2048], F32, name="ot")
+            for q in range(2):
+                for l in range(2):
+                    po = pp.tile([P, 512], F32, name="po")
+                    nc.tensor.matmul_mx(
+                        out=po[:],
+                        lhsT=ac[:, l * P : (l + 1) * P].bitcast(FP8X4),
+                        lhsT_scale=asc[:, l * P : (l + 1) * P],
+                        rhs=wc[:, q * 512 : (q + 1) * 512].bitcast(FP8X4),
+                        rhs_scale=ws[:, q * 512 : (q + 1) * 512],
+                        start=True,
+                        stop=True,
+                    )
+                    o0 = l * 1024 + q * 512
+                    nc.vector.tensor_tensor(
+                        out=ot[:, o0 : o0 + 512].rearrange("p (c a) -> p c a", a=4),
+                        in0=po[:].rearrange("p (a c) -> p c a", a=4),
+                        in1=bbs[i][:, q * 512 : (q + 1) * 512].rearrange("p (c a) -> p c a", a=4),
+                        op=ALU.add,
+                    )
+            nc.sync.dma_start(
+                out=out[b].rearrange("(m l) j -> m l j", l=2)[:, :, hb * 1024 : (hb + 1) * 1024],
+                in_=ot[:].rearrange("p (l j) -> p l j", l=2),
+            )
+
+        h_stage(0)
+        h_stage(1)
+        for i in range(UNITS):
+            b, hb = divmod(i, 2)
+            wt_stage(i)
+            if i == 0:
+                a_act(0)
+                a_regroup(0)
+            if i >= 1:
+                mm_stage(i - 1)
+            if i + WBUFS < UNITS:
+                load_w(i + WBUFS)
+            if hb == 0:
+                if b + 2 < NB:
+                    h_stage(b + 2)
+                a_quant(b)
+            else:
+                if b + 1 < NB:
+                    a_act(b + 1)
+                    a_regroup(b + 1)
+        mm_stage(UNITS - 1)

@@ -16,7 +16,8 @@ EPS = 1e-5
 P = 128
 FLOPS = 2 * NB * N * K * J
 UNITS = 2 * NB
-MANUAL = False
+MANUAL = True
+DUMMY_N = 0
 WBUFS = 8
 
 
@@ -37,6 +38,13 @@ def tile_decoder_pa_kernel(tc, h6_pre, g6, be6, W7, b7, out):
 
         ident = const.tile([P, P], F32, name="ident")
         make_identity(nc, ident[:])
+
+        def dummy(bank):
+            if DUMMY_N:
+                nc.tensor.matmul(
+                    out=bank[:, 0:DUMMY_N], lhsT=ident[:], rhs=ident[:, 0:DUMMY_N], start=True, stop=True
+                )
+
         mhalf = const.tile([P, 4], F32, name="mhalf")
         nc.gpsimd.memset(mhalf[:], -0.5)
         rows = const.tile([P, 2 * P], BF16, name="rows")
@@ -93,6 +101,7 @@ def tile_decoder_pa_kernel(tc, h6_pre, g6, be6, W7, b7, out):
 
         def h_stage(b):
             ht = tp.tile([P, 512], F32, name="ht", tag="tp")
+            dummy(ht)
             for u in range(2):
                 for l in range(2):
                     src = b * 512 + l * 256 + u * P
@@ -105,6 +114,9 @@ def tile_decoder_pa_kernel(tc, h6_pre, g6, be6, W7, b7, out):
             nc.scalar.copy(out=hT[:], in_=ht[:])
             hb16 = hT[:].bitcast(BF16)
             hts[b] = hb16
+
+        def h_stats(b):
+            hb16 = hts[b]
             for u in range(2):
                 nc.vector.bn_stats(
                     out=st[:, (b * 2 + u) * 6 : (b * 2 + u + 1) * 6],
@@ -154,6 +166,7 @@ def tile_decoder_pa_kernel(tc, h6_pre, g6, be6, W7, b7, out):
         def wt_stage(i):
             b, hb = divmod(i, 2)
             bt = tp.tile([P, 512], F32, name="bt", tag="tp")
+            dummy(bt)
             for s in range(4):
                 c = 32 + b * 8 + hb * 4 + s
                 nc.tensor.transpose(
@@ -171,6 +184,7 @@ def tile_decoder_pa_kernel(tc, h6_pre, g6, be6, W7, b7, out):
             for q in range(2):
                 for ap in range(2):
                     wt = tp.tile([P, 512], F32, name="wt", tag="tp")
+                    dummy(wt)
                     for al in range(2):
                         for u in range(2):
                             src = (q * 4 + 2 * ap + al) * 256 + u * P
@@ -219,10 +233,14 @@ def tile_decoder_pa_kernel(tc, h6_pre, g6, be6, W7, b7, out):
             )
 
         h_stage(0)
+        h_stats(0)
         h_stage(1)
+        h_stats(1)
         for i in range(UNITS):
             b, hb = divmod(i, 2)
             wt_stage(i)
+            if hb == 0 and b + 2 < NB:
+                h_stage(b + 2)
             if i == 0:
                 a_act(0)
                 a_regroup(0)
@@ -232,7 +250,7 @@ def tile_decoder_pa_kernel(tc, h6_pre, g6, be6, W7, b7, out):
                 load_w(i + WBUFS)
             if hb == 0:
                 if b + 2 < NB:
-                    h_stage(b + 2)
+                    h_stats(b + 2)
                 a_quant(b)
             else:
                 if b + 1 < NB:

@@ -17,7 +17,7 @@ P = 128
 FLOPS = 2 * NB * N * K * J
 UNITS = 2 * NB
 MANUAL = True
-DUMMY_N = 0
+DUMMY_N = 128
 WBUFS = 8
 
 

@@ -17,8 +17,9 @@ P = 128
 FLOPS = 2 * NB * N * K * J
 UNITS = 2 * NB
 MANUAL = True
-DUMMY_N = 128
+DUMMY_N = 96
 WBUFS = 8
+SPLIT_FROM = 14
 
 
 def tile_decoder_pa_kernel(tc, h6_pre, g6, be6, W7, b7, out):
@@ -74,10 +75,12 @@ def tile_decoder_pa_kernel(tc, h6_pre, g6, be6, W7, b7, out):
             wtiles[i] = wt
 
         load_h(0, 1)
-        load_w(0)
         load_h(1, 2)
+        load_h(2, 4)
+        load_w(0)
+        load_h(4, 6)
         load_w(1)
-        load_h(2, NB)
+        load_h(6, 8)
         for i in range(2, WBUFS):
             load_w(i)
 
@@ -227,33 +230,43 @@ def tile_decoder_pa_kernel(tc, h6_pre, g6, be6, W7, b7, out):
                         in1=bbs[i][:, q * 512 : (q + 1) * 512].rearrange("p (c a) -> p c a", a=4),
                         op=ALU.add,
                     )
-            nc.sync.dma_start(
-                out=out[b].rearrange("(m l) j -> m l j", l=2)[:, :, hb * 1024 : (hb + 1) * 1024],
-                in_=ot[:].rearrange("p (l j) -> p l j", l=2),
-            )
+                if i >= SPLIT_FROM:
+                    j0 = hb * 1024 + q * 512
+                    nc.sync.dma_start(
+                        out=out[b].rearrange("(m l) j -> m l j", l=2)[:, :, j0 : j0 + 512],
+                        in_=ot[:].rearrange("p (l j) -> p l j", l=2)[:, :, q * 512 : (q + 1) * 512],
+                    )
+            if i < SPLIT_FROM:
+                nc.sync.dma_start(
+                    out=out[b].rearrange("(m l) j -> m l j", l=2)[:, :, hb * 1024 : (hb + 1) * 1024],
+                    in_=ot[:].rearrange("p (l j) -> p l j", l=2),
+                )
 
-        h_stage(0)
-        h_stats(0)
-        h_stage(1)
-        h_stats(1)
-        for i in range(UNITS):
-            b, hb = divmod(i, 2)
+        for b in range(4):
+            h_stage(b)
+            h_stats(b)
+        wt_stage(0)
+        load_w(WBUFS)
+        a_act(0)
+        for b in range(4, 6):
+            h_stage(b)
+            h_stats(b)
+        a_regroup(0)
+        a_quant(0)
+        for i in range(1, UNITS):
             wt_stage(i)
-            if hb == 0 and b + 2 < NB:
-                h_stage(b + 2)
-            if i == 0:
-                a_act(0)
-                a_regroup(0)
-            if i >= 1:
-                mm_stage(i - 1)
+            if i == 2:
+                h_stage(6)
+                h_stage(7)
+            mm_stage(i - 1)
             if i + WBUFS < UNITS:
                 load_w(i + WBUFS)
-            if hb == 0:
-                if b + 2 < NB:
-                    h_stats(b + 2)
-                a_quant(b)
-            else:
-                if b + 1 < NB:
-                    a_act(b + 1)
-                    a_regroup(b + 1)
+            if i == 2:
+                h_stats(6)
+                h_stats(7)
+            if i % 2 == 1 and i < UNITS - 1:
+                a_act((i + 1) // 2)
+                a_regroup((i + 1) // 2)
+            if i % 2 == 0:
+                a_quant(i // 2)
         mm_stage(UNITS - 1)

@@ -16,10 +16,11 @@ EPS = 1e-5
 P = 128
 FLOPS = 2 * NB * N * K * J
 UNITS = 2 * NB
-MANUAL = True
-DUMMY_N = 96
+SUBS = 2 * UNITS
 WBUFS = 8
 SPLIT_FROM = 14
+LAG = 2
+S_TILES = ()
 
 
 def tile_decoder_pa_kernel(tc, h6_pre, g6, be6, W7, b7, out):
@@ -27,25 +28,17 @@ def tile_decoder_pa_kernel(tc, h6_pre, g6, be6, W7, b7, out):
     with ExitStack() as ctx:
         const = ctx.enter_context(tc.tile_pool(name="const", bufs=1))
         wpool = ctx.enter_context(tc.tile_pool(name="wload", bufs=WBUFS))
-        gpool = ctx.enter_context(tc.tile_pool(name="grouped", bufs=3))
-        cpool = ctx.enter_context(tc.tile_pool(name="codes", bufs=3))
+        gpool = ctx.enter_context(tc.tile_pool(name="grouped", bufs=6))
+        cpool = ctx.enter_context(tc.tile_pool(name="codes", bufs=6))
         apool = ctx.enter_context(tc.tile_pool(name="acts", bufs=2))
         bpool = ctx.enter_context(tc.tile_pool(name="bias", bufs=3))
         opool = ctx.enter_context(tc.tile_pool(name="outs", bufs=4))
         tp = ctx.enter_context(tc.psum_pool(name="tp", bufs=4))
         pp = ctx.enter_context(tc.psum_pool(name="pp", bufs=4))
-        if MANUAL:
-            ctx.enter_context(tc.manual_schedule())
+        ctx.enter_context(tc.manual_schedule())
 
         ident = const.tile([P, P], F32, name="ident")
         make_identity(nc, ident[:])
-
-        def dummy(bank):
-            if DUMMY_N:
-                nc.tensor.matmul(
-                    out=bank[:, 0:DUMMY_N], lhsT=ident[:], rhs=ident[:, 0:DUMMY_N], start=True, stop=True
-                )
-
         mhalf = const.tile([P, 4], F32, name="mhalf")
         nc.gpsimd.memset(mhalf[:], -0.5)
         rows = const.tile([P, 2 * P], BF16, name="rows")
@@ -104,7 +97,6 @@ def tile_decoder_pa_kernel(tc, h6_pre, g6, be6, W7, b7, out):
 
         def h_stage(b):
             ht = tp.tile([P, 512], F32, name="ht", tag="tp")
-            dummy(ht)
             for u in range(2):
                 for l in range(2):
                     src = b * 512 + l * 256 + u * P
@@ -115,8 +107,7 @@ def tile_decoder_pa_kernel(tc, h6_pre, g6, be6, W7, b7, out):
                     )
             hT = const.tile([P, 512], F32, name="hT%d" % b)
             nc.scalar.copy(out=hT[:], in_=ht[:])
-            hb16 = hT[:].bitcast(BF16)
-            hts[b] = hb16
+            hts[b] = hT[:].bitcast(BF16)
 
         def h_stats(b):
             hb16 = hts[b]
@@ -165,87 +156,95 @@ def tile_decoder_pa_kernel(tc, h6_pre, g6, be6, W7, b7, out):
 
         bbs = {}
         wcs = {}
+        ots = {}
 
-        def wt_stage(i):
+        def wt_stage(s):
+            i, q = divmod(s, 2)
             b, hb = divmod(i, 2)
-            bt = tp.tile([P, 512], F32, name="bt", tag="tp")
-            dummy(bt)
-            for s in range(4):
-                c = 32 + b * 8 + hb * 4 + s
-                nc.tensor.transpose(
-                    out=bt[:, s * P : (s + 1) * P],
-                    in_=cols[:, c : c + 1].to_broadcast([P, P]),
-                    identity=ident[:],
-                )
-            bb = bpool.tile([P, 512], F32, name="bb")
-            nc.scalar.copy(out=bb[:], in_=bt[:])
-            bbs[i] = bb[:].bitcast(BF16)
+            if q == 0:
+                bt = tp.tile([P, 512], F32, name="bt", tag="tp")
+                for r in range(4):
+                    c = 32 + b * 8 + hb * 4 + r
+                    nc.tensor.transpose(
+                        out=bt[:, r * P : (r + 1) * P],
+                        in_=cols[:, c : c + 1].to_broadcast([P, P]),
+                        identity=ident[:],
+                    )
+                bb = bpool.tile([P, 512], F32, name="bb")
+                nc.scalar.copy(out=bb[:], in_=bt[:])
+                bbs[i] = bb[:].bitcast(BF16)
 
             wf = wtiles[i][:].bitcast(F32)
-            gw = gpool.tile([P, 4096], BF16, name="gw", align_bytes=64)
+            gw = gpool.tile([P, 2048], BF16, name="gw", align_bytes=64)
             gwf = gw[:].bitcast(F32)
-            for q in range(2):
-                for ap in range(2):
-                    wt = tp.tile([P, 512], F32, name="wt", tag="tp")
-                    dummy(wt)
-                    for al in range(2):
-                        for u in range(2):
-                            src = (q * 4 + 2 * ap + al) * 256 + u * P
-                            nc.tensor.transpose(
-                                out=wt[:, (al * 2 + u) * P : (al * 2 + u + 1) * P],
-                                in_=wf[:, src : src + P],
-                                identity=ident[:],
-                            )
-                    base = (q * 512 + ap * 256) * 2
-                    nc.scalar.copy(
-                        out=gwf[:, base : base + 512].rearrange("p (a c u) -> p a c u", a=2, u=2),
-                        in_=wt[:].rearrange("p (a u c) -> p a c u", a=2, u=2),
-                    )
-            wc = cpool.tile([P, 1024], U32, name="wc", align_bytes=64)
-            ws = cpool.tile([P, 1024], U8, name="ws", align_bytes=64)
+            for ap in range(2):
+                wt = tp.tile([P, 512], F32, name="wt", tag="tp")
+                for al in range(2):
+                    for u in range(2):
+                        src = (q * 4 + 2 * ap + al) * 256 + u * P
+                        nc.tensor.transpose(
+                            out=wt[:, (al * 2 + u) * P : (al * 2 + u + 1) * P],
+                            in_=wf[:, src : src + P],
+                            identity=ident[:],
+                        )
+                nc.scalar.copy(
+                    out=gwf[:, ap * 512 : (ap + 1) * 512].rearrange("p (a c u) -> p a c u", a=2, u=2),
+                    in_=wt[:].rearrange("p (a u c) -> p a c u", a=2, u=2),
+                )
+            wc = cpool.tile([P, 512], U32, name="wc", align_bytes=64)
+            ws = cpool.tile([P, 512], U8, name="ws", align_bytes=64)
             nc.vector.quantize_mx(out=wc[:].bitcast(FP8X4), scales=ws[:], in_=gw[:])
-            wcs[i] = (wc, ws)
+            wcs[s] = (wc, ws)
 
-        def mm_stage(i):
+        def mm_stage(s):
+            i, q = divmod(s, 2)
             b, hb = divmod(i, 2)
             ac, asc = acs[b]
-            wc, ws = wcs[i]
-            ot = opool.tile([P, 2048], F32, name="ot")
-            for q in range(2):
-                for l in range(2):
-                    po = pp.tile([P, 512], F32, name="po")
-                    nc.tensor.matmul_mx(
-                        out=po[:],
-                        lhsT=ac[:, l * P : (l + 1) * P].bitcast(FP8X4),
-                        lhsT_scale=asc[:, l * P : (l + 1) * P],
-                        rhs=wc[:, q * 512 : (q + 1) * 512].bitcast(FP8X4),
-                        rhs_scale=ws[:, q * 512 : (q + 1) * 512],
-                        start=True,
-                        stop=True,
+            wc, ws = wcs[s]
+            if q == 0:
+                ots[i] = opool.tile([P, 2048], F32, name="ot")
+            ot = ots[i]
+            for l in range(2):
+                po = pp.tile([P, 512], F32, name="po")
+                nc.tensor.matmul_mx(
+                    out=po[:],
+                    lhsT=ac[:, l * P : (l + 1) * P].bitcast(FP8X4),
+                    lhsT_scale=asc[:, l * P : (l + 1) * P],
+                    rhs=wc[:].bitcast(FP8X4),
+                    rhs_scale=ws[:],
+                    start=True,
+                    stop=True,
+                )
+                o0 = l * 1024 + q * 512
+                bias = bbs[i][:, q * 512 : (q + 1) * 512]
+                if (s % 4, l) in S_TILES:
+                    nc.scalar.copy(
+                        out=ot[:, o0 : o0 + 512].rearrange("p (c a) -> p c a", a=4),
+                        in_=po[:].rearrange("p (a c) -> p c a", a=4),
                     )
-                    o0 = l * 1024 + q * 512
+                    nc.gpsimd.tensor_tensor(
+                        out=ot[:, o0 : o0 + 512], in0=ot[:, o0 : o0 + 512], in1=bias, op=ALU.add
+                    )
+                else:
                     nc.vector.tensor_tensor(
                         out=ot[:, o0 : o0 + 512].rearrange("p (c a) -> p c a", a=4),
                         in0=po[:].rearrange("p (a c) -> p c a", a=4),
-                        in1=bbs[i][:, q * 512 : (q + 1) * 512].rearrange("p (c a) -> p c a", a=4),
+                        in1=bias.rearrange("p (c a) -> p c a", a=4),
                         op=ALU.add,
                     )
-                if i >= SPLIT_FROM:
-                    j0 = hb * 1024 + q * 512
-                    nc.sync.dma_start(
-                        out=out[b].rearrange("(m l) j -> m l j", l=2)[:, :, j0 : j0 + 512],
-                        in_=ot[:].rearrange("p (l j) -> p l j", l=2)[:, :, q * 512 : (q + 1) * 512],
-                    )
-            if i < SPLIT_FROM:
-                nc.sync.dma_start(
-                    out=out[b].rearrange("(m l) j -> m l j", l=2)[:, :, hb * 1024 : (hb + 1) * 1024],
-                    in_=ot[:].rearrange("p (l j) -> p l j", l=2),
-                )
+            dst = out[b].rearrange("(m l) j -> m l j", l=2)
+            osrc = ot[:].rearrange("p (l j) -> p l j", l=2)
+            if i >= SPLIT_FROM:
+                j0 = hb * 1024 + q * 512
+                nc.sync.dma_start(out=dst[:, :, j0 : j0 + 512], in_=osrc[:, :, q * 512 : (q + 1) * 512])
+            elif q == 1:
+                nc.sync.dma_start(out=dst[:, :, hb * 1024 : (hb + 1) * 1024], in_=osrc)
 
         for b in range(4):
             h_stage(b)
             h_stats(b)
         wt_stage(0)
+        wt_stage(1)
         load_w(WBUFS)
         a_act(0)
         for b in range(4, 6):
@@ -253,20 +252,28 @@ def tile_decoder_pa_kernel(tc, h6_pre, g6, be6, W7, b7, out):
             h_stats(b)
         a_regroup(0)
         a_quant(0)
-        for i in range(1, UNITS):
-            wt_stage(i)
-            if i == 2:
+        for s in range(2, SUBS):
+            wt_stage(s)
+            if s == 4:
                 h_stage(6)
                 h_stage(7)
-            mm_stage(i - 1)
-            if i + WBUFS < UNITS:
-                load_w(i + WBUFS)
-            if i == 2:
+            mm_stage(s - LAG)
+            if s % 2 == 1 and s // 2 + WBUFS < UNITS:
+                load_w(s // 2 + WBUFS)
+            if s == 4:
                 h_stats(6)
                 h_stats(7)
-            if i % 2 == 1 and i < UNITS - 1:
-                a_act((i + 1) // 2)
-                a_regroup((i + 1) // 2)
-            if i % 2 == 0:
-                a_quant(i // 2)
-        mm_stage(UNITS - 1)
+            nxt = s // 4 + 1
+            step = s % 4
+            if s < 5:
+                nxt = 1
+                step = s - 1
+            if nxt < NB:
+                if step == 1:
+                    a_act(nxt)
+                if step == 2:
+                    a_regroup(nxt)
+                if step == 3:
+                    a_quant(nxt)
+        for s in range(SUBS - LAG, SUBS):
+            mm_stage(s)

@@ -20,7 +20,7 @@ SUBS = 2 * UNITS
 WBUFS = 8
 SPLIT_FROM = 14
 LAG = 2
-S_TILES = ()
+S_TILES = ((2, 0),)
 
 
 def tile_decoder_pa_kernel(tc, h6_pre, g6, be6, W7, b7, out):
@@ -232,37 +232,35 @@ def tile_decoder_pa_kernel(tc, h6_pre, g6, be6, W7, b7, out):
                         in1=bias.rearrange("p (c a) -> p c a", a=4),
                         op=ALU.add,
                     )
+                if s == SUBS - 1:
+                    nc.sync.dma_start(
+                        out=out[b].rearrange("(m l) j -> m l j", l=2)[:, l, hb * 1024 + 512 : hb * 1024 + 1024],
+                        in_=ot[:, o0 : o0 + 512],
+                    )
             dst = out[b].rearrange("(m l) j -> m l j", l=2)
             osrc = ot[:].rearrange("p (l j) -> p l j", l=2)
-            if i >= SPLIT_FROM:
+            if s < SUBS - 1 and i >= SPLIT_FROM:
                 j0 = hb * 1024 + q * 512
                 nc.sync.dma_start(out=dst[:, :, j0 : j0 + 512], in_=osrc[:, :, q * 512 : (q + 1) * 512])
-            elif q == 1:
+            if i < SPLIT_FROM and q == 1:
                 nc.sync.dma_start(out=dst[:, :, hb * 1024 : (hb + 1) * 1024], in_=osrc)
 
         for b in range(4):
             h_stage(b)
             h_stats(b)
         wt_stage(0)
-        wt_stage(1)
-        load_w(WBUFS)
         a_act(0)
-        for b in range(4, 6):
-            h_stage(b)
-            h_stats(b)
         a_regroup(0)
         a_quant(0)
+        wt_stage(1)
+        load_w(WBUFS)
         for s in range(2, SUBS):
             wt_stage(s)
-            if s == 4:
-                h_stage(6)
-                h_stage(7)
+            if s < 6:
+                h_stage(s + 2)
             mm_stage(s - LAG)
             if s % 2 == 1 and s // 2 + WBUFS < UNITS:
                 load_w(s // 2 + WBUFS)
-            if s == 4:
-                h_stats(6)
-                h_stats(7)
             nxt = s // 4 + 1
             step = s % 4
             if s < 5:
@@ -275,5 +273,7 @@ def tile_decoder_pa_kernel(tc, h6_pre, g6, be6, W7, b7, out):
                     a_regroup(nxt)
                 if step == 3:
                     a_quant(nxt)
+            if s < 6:
+                h_stats(s + 2)
         for s in range(SUBS - LAG, SUBS):
             mm_stage(s)

@@ -20,7 +20,7 @@ SUBS = 2 * UNITS
 WBUFS = 8
 SPLIT_FROM = 14
 LAG = 2
-S_TILES = ((2, 0),)
+S_TILES = ()
 
 
 def tile_decoder_pa_kernel(tc, h6_pre, g6, be6, W7, b7, out):

@@ -11,269 +11,279 @@ FP8X4 = mybir.dt.float8_e4m3fn_x4
 ACT = mybir.ActivationFunctionType
 ALU = mybir.AluOpType
 
-NB, N, K, J = 8, 256, 512, 2048
-EPS = 1e-5
 P = 128
-FLOPS = 2 * NB * N * K * J
-UNITS = 2 * NB
-SUBS = 2 * UNITS
-WBUFS = 8
-SPLIT_FROM = 14
+BLOCKS, ROWS, K, COLS = 8, 256, 512, 2048
+EPS = 1e-5
+FLOPS = 2 * BLOCKS * ROWS * K * COLS
+
+PACK = 4
+WORDS = K // 2
+BANK = 512
+STEP = 512
+HALF = 2 * STEP
+STEPS = BLOCKS * COLS // STEP
+HALVES = BLOCKS * COLS // HALF
+W_AHEAD = 8
 LAG = 2
-S_TILES = ()
+FINE_STORES = HALVES - 2
 
 
 def tile_decoder_pa_kernel(tc, h6_pre, g6, be6, W7, b7, out):
     nc = tc.nc
     with ExitStack() as ctx:
-        const = ctx.enter_context(tc.tile_pool(name="const", bufs=1))
-        wpool = ctx.enter_context(tc.tile_pool(name="wload", bufs=WBUFS))
-        gpool = ctx.enter_context(tc.tile_pool(name="grouped", bufs=6))
-        cpool = ctx.enter_context(tc.tile_pool(name="codes", bufs=6))
-        apool = ctx.enter_context(tc.tile_pool(name="acts", bufs=2))
-        bpool = ctx.enter_context(tc.tile_pool(name="bias", bufs=3))
-        opool = ctx.enter_context(tc.tile_pool(name="outs", bufs=4))
-        tp = ctx.enter_context(tc.psum_pool(name="tp", bufs=4))
-        pp = ctx.enter_context(tc.psum_pool(name="pp", bufs=4))
+        keep = ctx.enter_context(tc.tile_pool(name="keep", bufs=1))
+        w_pool = ctx.enter_context(tc.tile_pool(name="w_rows", bufs=W_AHEAD))
+        grouped_pool = ctx.enter_context(tc.tile_pool(name="w_grouped", bufs=6))
+        code_pool = ctx.enter_context(tc.tile_pool(name="w_codes", bufs=6))
+        a_pool = ctx.enter_context(tc.tile_pool(name="a_values", bufs=2))
+        bias_pool = ctx.enter_context(tc.tile_pool(name="bias", bufs=3))
+        out_pool = ctx.enter_context(tc.tile_pool(name="out_tiles", bufs=4))
+        flip_pool = ctx.enter_context(tc.psum_pool(name="flipped", bufs=4))
+        acc_pool = ctx.enter_context(tc.psum_pool(name="sums", bufs=4))
         ctx.enter_context(tc.manual_schedule())
 
-        ident = const.tile([P, P], F32, name="ident")
+        ident = keep.tile([P, P], F32, name="ident")
         make_identity(nc, ident[:])
-        mhalf = const.tile([P, 4], F32, name="mhalf")
-        nc.gpsimd.memset(mhalf[:], -0.5)
-        rows = const.tile([P, 2 * P], BF16, name="rows")
-        nc.vector.memset(rows[96:128, :], 0.0)
-        nc.sync.dma_start(out=rows[0:16, :], in_=g6.rearrange("b (u w) -> (b u) w", u=2))
-        nc.sync.dma_start(out=rows[16:32, :], in_=be6.rearrange("b (u w) -> (b u) w", u=2))
-        nc.sync.dma_start(out=rows[32:96, :], in_=b7.rearrange("b (c w) -> (b c) w", c=8))
+        minus_half = keep.tile([P, PACK], F32, name="minus_half")
+        nc.gpsimd.memset(minus_half[:], -0.5)
 
-        hs = const.tile([P, NB * 1024], BF16, name="hs")
-        hf = hs[:].bitcast(F32)
+        h_rows = keep.tile([P, BLOCKS * 2 * K], BF16, name="h_rows")
+        h_words = h_rows[:].bitcast(F32)
 
-        def load_h(b0, b1):
+        def load_h(first, last):
             nc.sync.dma_start(
-                out=hs[:, b0 * 1024 : b1 * 1024].rearrange("p (b l k) -> p b l k", l=2, k=K),
-                in_=h6_pre[b0:b1].rearrange("b (m l) k -> m b l k", l=2),
+                out=h_rows[:, first * 2 * K : last * 2 * K].rearrange("p (b l k) -> p b l k", l=2, k=K),
+                in_=h6_pre[first:last].rearrange("b (m l) k -> m b l k", l=2),
             )
 
-        wtiles = {}
+        w_rows = {}
 
-        def load_w(i):
-            b, hb = divmod(i, 2)
-            wt = wpool.tile([P, 4096], BF16, name="wsb")
+        def load_w(half):
+            b, side = divmod(half, 2)
+            tile = w_pool.tile([P, HALF * K // P], BF16, name="w_rows")
             nc.sync.dma_start(
-                out=wt[:].rearrange("p (q a k) -> p q a k", q=2, a=4),
-                in_=W7[b].rearrange("(q p a) k -> p q a k", q=4, p=P)[:, 2 * hb : 2 * hb + 2],
+                out=tile[:].rearrange("p (q a k) -> p q a k", q=2, a=4),
+                in_=W7[b].rearrange("(q c a) k -> c q a k", q=4, c=P)[:, 2 * side : 2 * side + 2],
             )
-            wtiles[i] = wt
+            w_rows[half] = tile
 
+        small_rows = keep.tile([P, 2 * P], BF16, name="small_rows")
+        nc.vector.memset(small_rows[96:128, :], 0.0)
         load_h(0, 1)
+        nc.sync.dma_start(out=small_rows[0:16, :], in_=g6.rearrange("b (u w) -> (b u) w", u=2))
+        nc.sync.dma_start(out=small_rows[16:32, :], in_=be6.rearrange("b (u w) -> (b u) w", u=2))
+        nc.sync.dma_start(out=small_rows[32:96, :], in_=b7.rearrange("b (c w) -> (b c) w", c=8))
         load_h(1, 2)
         load_h(2, 4)
         load_w(0)
         load_h(4, 6)
         load_w(1)
         load_h(6, 8)
-        for i in range(2, WBUFS):
-            load_w(i)
+        for half in range(2, W_AHEAD):
+            load_w(half)
 
-        ct = tp.tile([P, 512], F32, name="ct", tag="tp")
-        nc.tensor.transpose(out=ct[:, 0:P], in_=rows[:].bitcast(F32), identity=ident[:])
-        cols = const.tile([P, P], F32, name="cols")
-        nc.scalar.copy(out=cols[:], in_=ct[:, 0:P])
-        colsb = cols[:].bitcast(BF16)
+        stats = keep.tile([P, BLOCKS * PACK * 3], F32, name="stats")
+        stats_view = stats[:].rearrange("p (i c) -> p i c", c=3)
+        var_eps = keep.tile([P, BLOCKS * PACK], F32, name="var_eps")
+        inv_std = keep.tile([P, BLOCKS * PACK], F32, name="inv_std")
+        scale = keep.tile([P, BLOCKS * PACK], F32, name="scale")
+        mean_scaled = keep.tile([P, BLOCKS * PACK], F32, name="mean_scaled")
+        shift = keep.tile([P, BLOCKS * PACK], F32, name="shift")
+        small_cols = keep.tile([P, P], F32, name="small_cols")
+        small_values = small_cols[:].bitcast(BF16)
+        h_flipped = {}
+        a_planes = {}
+        a_grouped = {}
+        a_codes = {}
 
-        st = const.tile([P, NB * 12], F32, name="st")
-        stv = st[:].rearrange("p (i c) -> p i c", c=3)
-        vv = const.tile([P, NB * 4], F32, name="vv")
-        rr = const.tile([P, NB * 4], F32, name="rr")
-        sc = const.tile([P, NB * 4], F32, name="sc")
-        ms = const.tile([P, NB * 4], F32, name="ms")
-        sh = const.tile([P, NB * 4], F32, name="sh")
-        hts = {}
-        ats = {}
-        ags = {}
-        acs = {}
-
-        def h_stage(b):
-            ht = tp.tile([P, 512], F32, name="ht", tag="tp")
+        def transpose_h(b):
+            bank = flip_pool.tile([P, BANK], F32, name="bank", tag="bank")
             for u in range(2):
                 for l in range(2):
-                    src = b * 512 + l * 256 + u * P
+                    first = (b * 2 + l) * WORDS + u * P
                     nc.tensor.transpose(
-                        out=ht[:, (u * 2 + l) * P : (u * 2 + l + 1) * P],
-                        in_=hf[:, src : src + P],
+                        out=bank[:, (u * 2 + l) * P : (u * 2 + l + 1) * P],
+                        in_=h_words[:, first : first + P],
                         identity=ident[:],
                     )
-            hT = const.tile([P, 512], F32, name="hT%d" % b)
-            nc.scalar.copy(out=hT[:], in_=ht[:])
-            hts[b] = hT[:].bitcast(BF16)
+            flipped = keep.tile([P, BANK], F32, name="h_flipped%d" % b)
+            nc.scalar.copy(out=flipped[:], in_=bank[:])
+            h_flipped[b] = flipped[:].bitcast(BF16)
 
-        def h_stats(b):
-            hb16 = hts[b]
+        def transpose_small():
+            bank = flip_pool.tile([P, BANK], F32, name="bank", tag="bank")
+            nc.tensor.transpose(out=bank[:, 0:P], in_=small_rows[:].bitcast(F32), identity=ident[:])
+            nc.scalar.copy(out=small_cols[:], in_=bank[:, 0:P])
+
+        def statistics(b):
             for u in range(2):
                 nc.vector.bn_stats(
-                    out=st[:, (b * 2 + u) * 6 : (b * 2 + u + 1) * 6],
-                    in_=hb16[:, u * 512 : (u + 1) * 512],
+                    out=stats[:, (b * 2 + u) * 6 : (b * 2 + u + 1) * 6],
+                    in_=h_flipped[b][:, u * 2 * ROWS : (u + 1) * 2 * ROWS],
                 )
-            i0, i1 = 4 * b, 4 * b + 4
+            four = slice(PACK * b, PACK * b + PACK)
             nc.gpsimd.tensor_scalar(
-                out=vv[:, i0:i1], in0=stv[:, i0:i1, 2], scalar1=1.0 / N, scalar2=EPS,
+                out=var_eps[:, four], in0=stats_view[:, four, 2], scalar1=1.0 / ROWS, scalar2=EPS,
                 op0=ALU.mult, op1=ALU.add,
             )
-            nc.gpsimd.tensor_tensor(out=rr[:, i0:i1], in0=vv[:, i0:i1], in1=mhalf[:], op=ALU.pow)
-            nc.gpsimd.tensor_tensor(out=sc[:, i0:i1], in0=rr[:, i0:i1], in1=colsb[:, i0:i1], op=ALU.mult)
-            nc.gpsimd.tensor_tensor(out=ms[:, i0:i1], in0=stv[:, i0:i1, 1], in1=sc[:, i0:i1], op=ALU.mult)
+            nc.gpsimd.tensor_tensor(out=inv_std[:, four], in0=var_eps[:, four], in1=minus_half[:], op=ALU.pow)
+            nc.gpsimd.tensor_tensor(out=scale[:, four], in0=inv_std[:, four], in1=small_values[:, four], op=ALU.mult)
             nc.gpsimd.tensor_tensor(
-                out=sh[:, i0:i1], in0=colsb[:, 32 + i0 : 32 + i1], in1=ms[:, i0:i1], op=ALU.subtract
+                out=mean_scaled[:, four], in0=stats_view[:, four, 1], in1=scale[:, four], op=ALU.mult
+            )
+            nc.gpsimd.tensor_tensor(
+                out=shift[:, four],
+                in0=small_values[:, BLOCKS * PACK + PACK * b : BLOCKS * PACK + PACK * b + PACK],
+                in1=mean_scaled[:, four],
+                op=ALU.subtract,
             )
 
-        def a_act(b):
-            at = apool.tile([P, 1024], BF16, name="at")
+        def normalise(b):
+            planes = a_pool.tile([P, PACK * ROWS], BF16, name="a_planes")
             for u in range(2):
-                pairs = hts[b][:, u * 512 : (u + 1) * 512].rearrange("p (n e) -> p n e", e=2)
+                pairs = h_flipped[b][:, u * 2 * ROWS : (u + 1) * 2 * ROWS].rearrange("p (n e) -> p n e", e=2)
                 for e in range(2):
                     t = 2 * u + e
                     nc.scalar.activation(
-                        out=at[:, t * N : (t + 1) * N], in_=pairs[:, :, e], func=ACT.Relu,
-                        scale=sc[:, 4 * b + t : 4 * b + t + 1], bias=sh[:, 4 * b + t : 4 * b + t + 1],
+                        out=planes[:, t * ROWS : (t + 1) * ROWS],
+                        in_=pairs[:, :, e],
+                        func=ACT.Relu,
+                        scale=scale[:, PACK * b + t : PACK * b + t + 1],
+                        bias=shift[:, PACK * b + t : PACK * b + t + 1],
                     )
-            ats[b] = at
+            a_planes[b] = planes
 
-        def a_regroup(b):
-            ag = apool.tile([P, 1024], BF16, name="ag", align_bytes=64)
-            nc.vector.tensor_copy(
-                out=ag[:].rearrange("p (c i t) -> p c t i", i=4, t=4),
-                in_=ats[b][:].rearrange("p (t c i) -> p c t i", t=4, i=4),
+        def regroup(b):
+            grouped = a_pool.tile([P, ROWS * PACK], BF16, name="a_grouped", align_bytes=64)
+            copy = nc.scalar.copy if b % 2 == 1 else nc.vector.tensor_copy
+            copy(
+                out=grouped[:].rearrange("p (c i t) -> p c t i", i=4, t=PACK),
+                in_=a_planes[b][:].rearrange("p (t c i) -> p c t i", t=PACK, i=4),
             )
-            ags[b] = ag
+            a_grouped[b] = grouped
 
-        def a_quant(b):
-            ac = const.tile([P, N], U32, name="ac%d" % b, align_bytes=64)
-            asc = const.tile([P, N], U8, name="as%d" % b, align_bytes=64)
-            nc.vector.quantize_mx(out=ac[:].bitcast(FP8X4), scales=asc[:], in_=ags[b][:])
-            acs[b] = (ac, asc)
+        def quantise_a(b):
+            codes = keep.tile([P, ROWS], U32, name="a_codes%d" % b, align_bytes=64)
+            scales = keep.tile([P, ROWS], U8, name="a_scales%d" % b, align_bytes=64)
+            nc.vector.quantize_mx(out=codes[:].bitcast(FP8X4), scales=scales[:], in_=a_grouped[b][:])
+            a_codes[b] = (codes, scales)
 
-        bbs = {}
-        wcs = {}
-        ots = {}
+        bias_tiles = {}
+        w_grouped = {}
+        w_codes = {}
+        out_tiles = {}
 
-        def wt_stage(s):
-            i, q = divmod(s, 2)
-            b, hb = divmod(i, 2)
+        def spread_bias(half):
+            bank = flip_pool.tile([P, BANK], F32, name="bank", tag="bank")
+            for r in range(4):
+                column = 32 + 4 * half + r
+                nc.tensor.transpose(
+                    out=bank[:, r * P : (r + 1) * P],
+                    in_=small_cols[:, column : column + 1].to_broadcast([P, P]),
+                    identity=ident[:],
+                )
+            spread = bias_pool.tile([P, BANK], F32, name="bias")
+            nc.scalar.copy(out=spread[:], in_=bank[:])
+            bias_tiles[half] = spread[:].bitcast(BF16)
+
+        def transpose_w(step, copy):
+            half, q = divmod(step, 2)
             if q == 0:
-                bt = tp.tile([P, 512], F32, name="bt", tag="tp")
-                for r in range(4):
-                    c = 32 + b * 8 + hb * 4 + r
-                    nc.tensor.transpose(
-                        out=bt[:, r * P : (r + 1) * P],
-                        in_=cols[:, c : c + 1].to_broadcast([P, P]),
-                        identity=ident[:],
-                    )
-                bb = bpool.tile([P, 512], F32, name="bb")
-                nc.scalar.copy(out=bb[:], in_=bt[:])
-                bbs[i] = bb[:].bitcast(BF16)
-
-            wf = wtiles[i][:].bitcast(F32)
-            gw = gpool.tile([P, 2048], BF16, name="gw", align_bytes=64)
-            gwf = gw[:].bitcast(F32)
-            for ap in range(2):
-                wt = tp.tile([P, 512], F32, name="wt", tag="tp")
-                for al in range(2):
+                spread_bias(half)
+            words = w_rows[half][:].bitcast(F32)
+            grouped = grouped_pool.tile([P, STEP * PACK], BF16, name="w_grouped", align_bytes=64)
+            grouped_words = grouped[:].bitcast(F32)
+            for pair in range(2):
+                bank = flip_pool.tile([P, BANK], F32, name="bank", tag="bank")
+                for a in range(2):
                     for u in range(2):
-                        src = (q * 4 + 2 * ap + al) * 256 + u * P
+                        first = (q * 4 + 2 * pair + a) * WORDS + u * P
                         nc.tensor.transpose(
-                            out=wt[:, (al * 2 + u) * P : (al * 2 + u + 1) * P],
-                            in_=wf[:, src : src + P],
+                            out=bank[:, (a * 2 + u) * P : (a * 2 + u + 1) * P],
+                            in_=words[:, first : first + P],
                             identity=ident[:],
                         )
-                nc.scalar.copy(
-                    out=gwf[:, ap * 512 : (ap + 1) * 512].rearrange("p (a c u) -> p a c u", a=2, u=2),
-                    in_=wt[:].rearrange("p (a u c) -> p a c u", a=2, u=2),
+                copy(
+                    out=grouped_words[:, pair * BANK : (pair + 1) * BANK].rearrange("p (a c u) -> p a c u", a=2, u=2),
+                    in_=bank[:].rearrange("p (a u c) -> p a c u", a=2, u=2),
                 )
-            wc = cpool.tile([P, 512], U32, name="wc", align_bytes=64)
-            ws = cpool.tile([P, 512], U8, name="ws", align_bytes=64)
-            nc.vector.quantize_mx(out=wc[:].bitcast(FP8X4), scales=ws[:], in_=gw[:])
-            wcs[s] = (wc, ws)
+            w_grouped[step] = grouped
 
-        def mm_stage(s):
-            i, q = divmod(s, 2)
-            b, hb = divmod(i, 2)
-            ac, asc = acs[b]
-            wc, ws = wcs[s]
+        def quantise_w(step):
+            codes = code_pool.tile([P, STEP], U32, name="w_codes", align_bytes=64)
+            scales = code_pool.tile([P, STEP], U8, name="w_scales", align_bytes=64)
+            nc.vector.quantize_mx(out=codes[:].bitcast(FP8X4), scales=scales[:], in_=w_grouped[step][:])
+            w_codes[step] = (codes, scales)
+
+        def multiply(step):
+            half, q = divmod(step, 2)
+            b, side = divmod(half, 2)
+            codes, scales = a_codes[b]
+            moving, moving_scales = w_codes[step]
             if q == 0:
-                ots[i] = opool.tile([P, 2048], F32, name="ot")
-            ot = ots[i]
+                out_tiles[half] = out_pool.tile([P, 2 * HALF], F32, name="out_tile")
+            tile = out_tiles[half]
+            rows = out[b].rearrange("(m l) j -> m l j", l=2)
+            first_col = side * HALF + q * STEP
             for l in range(2):
-                po = pp.tile([P, 512], F32, name="po")
+                acc = acc_pool.tile([P, BANK], F32, name="acc")
                 nc.tensor.matmul_mx(
-                    out=po[:],
-                    lhsT=ac[:, l * P : (l + 1) * P].bitcast(FP8X4),
-                    lhsT_scale=asc[:, l * P : (l + 1) * P],
-                    rhs=wc[:].bitcast(FP8X4),
-                    rhs_scale=ws[:],
+                    out=acc[:],
+                    lhsT=codes[:, l * P : (l + 1) * P].bitcast(FP8X4),
+                    lhsT_scale=scales[:, l * P : (l + 1) * P],
+                    rhs=moving[:].bitcast(FP8X4),
+                    rhs_scale=moving_scales[:],
                     start=True,
                     stop=True,
                 )
-                o0 = l * 1024 + q * 512
-                bias = bbs[i][:, q * 512 : (q + 1) * 512]
-                if (s % 4, l) in S_TILES:
-                    nc.scalar.copy(
-                        out=ot[:, o0 : o0 + 512].rearrange("p (c a) -> p c a", a=4),
-                        in_=po[:].rearrange("p (a c) -> p c a", a=4),
-                    )
-                    nc.gpsimd.tensor_tensor(
-                        out=ot[:, o0 : o0 + 512], in0=ot[:, o0 : o0 + 512], in1=bias, op=ALU.add
-                    )
-                else:
-                    nc.vector.tensor_tensor(
-                        out=ot[:, o0 : o0 + 512].rearrange("p (c a) -> p c a", a=4),
-                        in0=po[:].rearrange("p (a c) -> p c a", a=4),
-                        in1=bias.rearrange("p (c a) -> p c a", a=4),
-                        op=ALU.add,
-                    )
-                if s == SUBS - 1:
-                    nc.sync.dma_start(
-                        out=out[b].rearrange("(m l) j -> m l j", l=2)[:, l, hb * 1024 + 512 : hb * 1024 + 1024],
-                        in_=ot[:, o0 : o0 + 512],
-                    )
-            dst = out[b].rearrange("(m l) j -> m l j", l=2)
-            osrc = ot[:].rearrange("p (l j) -> p l j", l=2)
-            if s < SUBS - 1 and i >= SPLIT_FROM:
-                j0 = hb * 1024 + q * 512
-                nc.sync.dma_start(out=dst[:, :, j0 : j0 + 512], in_=osrc[:, :, q * 512 : (q + 1) * 512])
-            if i < SPLIT_FROM and q == 1:
-                nc.sync.dma_start(out=dst[:, :, hb * 1024 : (hb + 1) * 1024], in_=osrc)
+                part = tile[:, l * HALF + q * STEP : l * HALF + (q + 1) * STEP]
+                nc.vector.tensor_tensor(
+                    out=part.rearrange("p (c a) -> p c a", a=4),
+                    in0=acc[:].rearrange("p (a c) -> p c a", a=4),
+                    in1=bias_tiles[half][:, q * STEP : (q + 1) * STEP].rearrange("p (c a) -> p c a", a=4),
+                    op=ALU.add,
+                )
+                if step == STEPS - 1:
+                    nc.sync.dma_start(out=rows[:, l, first_col : first_col + STEP], in_=part)
+            both = tile[:].rearrange("p (l j) -> p l j", l=2)
+            if half >= FINE_STORES and step < STEPS - 1:
+                nc.sync.dma_start(
+                    out=rows[:, :, first_col : first_col + STEP], in_=both[:, :, q * STEP : (q + 1) * STEP]
+                )
+            if half < FINE_STORES and q == 1:
+                nc.sync.dma_start(out=rows[:, :, side * HALF : (side + 1) * HALF], in_=both)
 
-        for b in range(4):
-            h_stage(b)
-            h_stats(b)
-        wt_stage(0)
-        a_act(0)
-        a_regroup(0)
-        a_quant(0)
-        wt_stage(1)
-        load_w(WBUFS)
-        for s in range(2, SUBS):
-            wt_stage(s)
-            if s < 6:
-                h_stage(s + 2)
-            mm_stage(s - LAG)
-            if s % 2 == 1 and s // 2 + WBUFS < UNITS:
-                load_w(s // 2 + WBUFS)
-            nxt = s // 4 + 1
-            step = s % 4
-            if s < 5:
-                nxt = 1
-                step = s - 1
-            if nxt < NB:
-                if step == 1:
-                    a_act(nxt)
-                if step == 2:
-                    a_regroup(nxt)
-                if step == 3:
-                    a_quant(nxt)
-            if s < 6:
-                h_stats(s + 2)
-        for s in range(SUBS - LAG, SUBS):
-            mm_stage(s)
+        transpose_h(0)
+        transpose_small()
+        statistics(0)
+        for b in range(1, 4):
+            transpose_h(b)
+            statistics(b)
+        transpose_w(0, nc.scalar.copy)
+        quantise_w(0)
+        normalise(0)
+        transpose_w(1, nc.vector.tensor_copy)
+        load_w(W_AHEAD)
+        regroup(0)
+        quantise_a(0)
+        quantise_w(1)
+        prepare_from = [max(2, 4 * b - 3) for b in range(BLOCKS)]
+        for step in range(2, STEPS):
+            transpose_w(step, nc.scalar.copy)
+            quantise_w(step)
+            if step < 6:
+                transpose_h(step + 2)
+            multiply(step - LAG)
+            if step % 2 == 1 and step // 2 + W_AHEAD < HALVES:
+                load_w(step // 2 + W_AHEAD)
+            for b in range(1, BLOCKS):
+                if step == prepare_from[b]:
+                    normalise(b)
+                if step == prepare_from[b] + 1:
+                    regroup(b)
+                if step == prepare_from[b] + 2:
+                    quantise_a(b)
+            if step < 6:
+                statistics(step + 2)
+        for step in range(STEPS - LAG, STEPS):
+            multiply(step)

from contextlib import ExitStack

import concourse.mybir as mybir
from concourse.masks import make_identity

F32 = mybir.dt.float32
BF16 = mybir.dt.bfloat16
U32 = mybir.dt.uint32
U8 = mybir.dt.uint8
FP8X4 = mybir.dt.float8_e4m3fn_x4
ACT = mybir.ActivationFunctionType
ALU = mybir.AluOpType

P = 128
BLOCKS, ROWS, K, COLS = 8, 256, 512, 2048
EPS = 1e-5
FLOPS = 2 * BLOCKS * ROWS * K * COLS

PACK = 4
WORDS = K // 2
BANK = 512
STEP = 512
HALF = 2 * STEP
STEPS = BLOCKS * COLS // STEP
HALVES = BLOCKS * COLS // HALF
W_AHEAD = 8
LAG = 2
FINE_STORES = HALVES - 2


def tile_decoder_pa_kernel(tc, h6_pre, g6, be6, W7, b7, out):
    nc = tc.nc
    with ExitStack() as ctx:
        keep = ctx.enter_context(tc.tile_pool(name="keep", bufs=1))
        w_pool = ctx.enter_context(tc.tile_pool(name="w_rows", bufs=W_AHEAD))
        grouped_pool = ctx.enter_context(tc.tile_pool(name="w_grouped", bufs=6))
        code_pool = ctx.enter_context(tc.tile_pool(name="w_codes", bufs=6))
        a_pool = ctx.enter_context(tc.tile_pool(name="a_values", bufs=2))
        bias_pool = ctx.enter_context(tc.tile_pool(name="bias", bufs=3))
        out_pool = ctx.enter_context(tc.tile_pool(name="out_tiles", bufs=4))
        flip_pool = ctx.enter_context(tc.psum_pool(name="flipped", bufs=4))
        acc_pool = ctx.enter_context(tc.psum_pool(name="sums", bufs=4))
        ctx.enter_context(tc.manual_schedule())

        ident = keep.tile([P, P], F32, name="ident")
        make_identity(nc, ident[:])
        minus_half = keep.tile([P, PACK], F32, name="minus_half")
        nc.gpsimd.memset(minus_half[:], -0.5)

        h_rows = keep.tile([P, BLOCKS * 2 * K], BF16, name="h_rows")
        h_words = h_rows[:].bitcast(F32)

        def load_h(first, last):
            nc.sync.dma_start(
                out=h_rows[:, first * 2 * K : last * 2 * K].rearrange("p (b l k) -> p b l k", l=2, k=K),
                in_=h6_pre[first:last].rearrange("b (m l) k -> m b l k", l=2),
            )

        w_rows = {}

        def load_w(half):
            b, side = divmod(half, 2)
            tile = w_pool.tile([P, HALF * K // P], BF16, name="w_rows")
            nc.sync.dma_start(
                out=tile[:].rearrange("p (q a k) -> p q a k", q=2, a=4),
                in_=W7[b].rearrange("(q c a) k -> c q a k", q=4, c=P)[:, 2 * side : 2 * side + 2],
            )
            w_rows[half] = tile

        small_rows = keep.tile([P, 2 * P], BF16, name="small_rows")
        nc.vector.memset(small_rows[96:128, :], 0.0)
        load_h(0, 1)
        nc.sync.dma_start(out=small_rows[0:16, :], in_=g6.rearrange("b (u w) -> (b u) w", u=2))
        nc.sync.dma_start(out=small_rows[16:32, :], in_=be6.rearrange("b (u w) -> (b u) w", u=2))
        nc.sync.dma_start(out=small_rows[32:96, :], in_=b7.rearrange("b (c w) -> (b c) w", c=8))
        load_h(1, 2)
        load_h(2, 4)
        load_w(0)
        load_h(4, 6)
        load_w(1)
        load_h(6, 8)
        for half in range(2, W_AHEAD):
            load_w(half)

        stats = keep.tile([P, BLOCKS * PACK * 3], F32, name="stats")
        stats_view = stats[:].rearrange("p (i c) -> p i c", c=3)
        var_eps = keep.tile([P, BLOCKS * PACK], F32, name="var_eps")
        inv_std = keep.tile([P, BLOCKS * PACK], F32, name="inv_std")
        scale = keep.tile([P, BLOCKS * PACK], F32, name="scale")
        mean_scaled = keep.tile([P, BLOCKS * PACK], F32, name="mean_scaled")
        shift = keep.tile([P, BLOCKS * PACK], F32, name="shift")
        small_cols = keep.tile([P, P], F32, name="small_cols")
        small_values = small_cols[:].bitcast(BF16)
        h_flipped = {}
        a_planes = {}
        a_grouped = {}
        a_codes = {}

        def transpose_h(b):
            bank = flip_pool.tile([P, BANK], F32, name="bank", tag="bank")
            for u in range(2):
                for l in range(2):
                    first = (b * 2 + l) * WORDS + u * P
                    nc.tensor.transpose(
                        out=bank[:, (u * 2 + l) * P : (u * 2 + l + 1) * P],
                        in_=h_words[:, first : first + P],
                        identity=ident[:],
                    )
            flipped = keep.tile([P, BANK], F32, name="h_flipped%d" % b)
            nc.scalar.copy(out=flipped[:], in_=bank[:])
            h_flipped[b] = flipped[:].bitcast(BF16)

        def transpose_small():
            bank = flip_pool.tile([P, BANK], F32, name="bank", tag="bank")
            nc.tensor.transpose(out=bank[:, 0:P], in_=small_rows[:].bitcast(F32), identity=ident[:])
            nc.scalar.copy(out=small_cols[:], in_=bank[:, 0:P])

        def statistics(b):
            for u in range(2):
                nc.vector.bn_stats(
                    out=stats[:, (b * 2 + u) * 6 : (b * 2 + u + 1) * 6],
                    in_=h_flipped[b][:, u * 2 * ROWS : (u + 1) * 2 * ROWS],
                )
            four = slice(PACK * b, PACK * b + PACK)
            nc.gpsimd.tensor_scalar(
                out=var_eps[:, four], in0=stats_view[:, four, 2], scalar1=1.0 / ROWS, scalar2=EPS,
                op0=ALU.mult, op1=ALU.add,
            )
            nc.gpsimd.tensor_tensor(out=inv_std[:, four], in0=var_eps[:, four], in1=minus_half[:], op=ALU.pow)
            nc.gpsimd.tensor_tensor(out=scale[:, four], in0=inv_std[:, four], in1=small_values[:, four], op=ALU.mult)
            nc.gpsimd.tensor_tensor(
                out=mean_scaled[:, four], in0=stats_view[:, four, 1], in1=scale[:, four], op=ALU.mult
            )
            nc.gpsimd.tensor_tensor(
                out=shift[:, four],
                in0=small_values[:, BLOCKS * PACK + PACK * b : BLOCKS * PACK + PACK * b + PACK],
                in1=mean_scaled[:, four],
                op=ALU.subtract,
            )

        def normalise(b):
            planes = a_pool.tile([P, PACK * ROWS], BF16, name="a_planes")
            for u in range(2):
                pairs = h_flipped[b][:, u * 2 * ROWS : (u + 1) * 2 * ROWS].rearrange("p (n e) -> p n e", e=2)
                for e in range(2):
                    t = 2 * u + e
                    nc.scalar.activation(
                        out=planes[:, t * ROWS : (t + 1) * ROWS],
                        in_=pairs[:, :, e],
                        func=ACT.Relu,
                        scale=scale[:, PACK * b + t : PACK * b + t + 1],
                        bias=shift[:, PACK * b + t : PACK * b + t + 1],
                    )
            a_planes[b] = planes

        def regroup(b):
            grouped = a_pool.tile([P, ROWS * PACK], BF16, name="a_grouped", align_bytes=64)
            copy = nc.scalar.copy if b % 2 == 1 else nc.vector.tensor_copy
            copy(
                out=grouped[:].rearrange("p (c i t) -> p c t i", i=4, t=PACK),
                in_=a_planes[b][:].rearrange("p (t c i) -> p c t i", t=PACK, i=4),
            )
            a_grouped[b] = grouped

        def quantise_a(b):
            codes = keep.tile([P, ROWS], U32, name="a_codes%d" % b, align_bytes=64)
            scales = keep.tile([P, ROWS], U8, name="a_scales%d" % b, align_bytes=64)
            nc.vector.quantize_mx(out=codes[:].bitcast(FP8X4), scales=scales[:], in_=a_grouped[b][:])
            a_codes[b] = (codes, scales)

        bias_tiles = {}
        w_grouped = {}
        w_codes = {}
        out_tiles = {}

        def spread_bias(half):
            bank = flip_pool.tile([P, BANK], F32, name="bank", tag="bank")
            for r in range(4):
                column = 32 + 4 * half + r
                nc.tensor.transpose(
                    out=bank[:, r * P : (r + 1) * P],
                    in_=small_cols[:, column : column + 1].to_broadcast([P, P]),
                    identity=ident[:],
                )
            spread = bias_pool.tile([P, BANK], F32, name="bias")
            nc.scalar.copy(out=spread[:], in_=bank[:])
            bias_tiles[half] = spread[:].bitcast(BF16)

        def transpose_w(step, copy):
            half, q = divmod(step, 2)
            if q == 0:
                spread_bias(half)
            words = w_rows[half][:].bitcast(F32)
            grouped = grouped_pool.tile([P, STEP * PACK], BF16, name="w_grouped", align_bytes=64)
            grouped_words = grouped[:].bitcast(F32)
            for pair in range(2):
                bank = flip_pool.tile([P, BANK], F32, name="bank", tag="bank")
                for a in range(2):
                    for u in range(2):
                        first = (q * 4 + 2 * pair + a) * WORDS + u * P
                        nc.tensor.transpose(
                            out=bank[:, (a * 2 + u) * P : (a * 2 + u + 1) * P],
                            in_=words[:, first : first + P],
                            identity=ident[:],
                        )
                copy(
                    out=grouped_words[:, pair * BANK : (pair + 1) * BANK].rearrange("p (a c u) -> p a c u", a=2, u=2),
                    in_=bank[:].rearrange("p (a u c) -> p a c u", a=2, u=2),
                )
            w_grouped[step] = grouped

        def quantise_w(step):
            codes = code_pool.tile([P, STEP], U32, name="w_codes", align_bytes=64)
            scales = code_pool.tile([P, STEP], U8, name="w_scales", align_bytes=64)
            nc.vector.quantize_mx(out=codes[:].bitcast(FP8X4), scales=scales[:], in_=w_grouped[step][:])
            w_codes[step] = (codes, scales)

        def multiply(step):
            half, q = divmod(step, 2)
            b, side = divmod(half, 2)
            codes, scales = a_codes[b]
            moving, moving_scales = w_codes[step]
            if q == 0:
                out_tiles[half] = out_pool.tile([P, 2 * HALF], F32, name="out_tile")
            tile = out_tiles[half]
            rows = out[b].rearrange("(m l) j -> m l j", l=2)
            first_col = side * HALF + q * STEP
            for l in range(2):
                acc = acc_pool.tile([P, BANK], F32, name="acc")
                nc.tensor.matmul_mx(
                    out=acc[:],
                    lhsT=codes[:, l * P : (l + 1) * P].bitcast(FP8X4),
                    lhsT_scale=scales[:, l * P : (l + 1) * P],
                    rhs=moving[:].bitcast(FP8X4),
                    rhs_scale=moving_scales[:],
                    start=True,
                    stop=True,
                )
                part = tile[:, l * HALF + q * STEP : l * HALF + (q + 1) * STEP]
                nc.vector.tensor_tensor(
                    out=part.rearrange("p (c a) -> p c a", a=4),
                    in0=acc[:].rearrange("p (a c) -> p c a", a=4),
                    in1=bias_tiles[half][:, q * STEP : (q + 1) * STEP].rearrange("p (c a) -> p c a", a=4),
                    op=ALU.add,
                )
                if step == STEPS - 1:
                    nc.sync.dma_start(out=rows[:, l, first_col : first_col + STEP], in_=part)
            both = tile[:].rearrange("p (l j) -> p l j", l=2)
            if half >= FINE_STORES and step < STEPS - 1:
                nc.sync.dma_start(
                    out=rows[:, :, first_col : first_col + STEP], in_=both[:, :, q * STEP : (q + 1) * STEP]
                )
            if half < FINE_STORES and q == 1:
                nc.sync.dma_start(out=rows[:, :, side * HALF : (side + 1) * HALF], in_=both)

        transpose_h(0)
        transpose_small()
        statistics(0)
        for b in range(1, 4):
            transpose_h(b)
            statistics(b)
        transpose_w(0, nc.scalar.copy)
        quantise_w(0)
        normalise(0)
        transpose_w(1, nc.vector.tensor_copy)
        load_w(W_AHEAD)
        regroup(0)
        quantise_a(0)
        quantise_w(1)
        prepare_from = [max(2, 4 * b - 3) for b in range(BLOCKS)]
        for step in range(2, STEPS):
            transpose_w(step, nc.scalar.copy)
            quantise_w(step)
            if step < 6:
                transpose_h(step + 2)
            multiply(step - LAG)
            if step % 2 == 1 and step // 2 + W_AHEAD < HALVES:
                load_w(step // 2 + W_AHEAD)
            for b in range(1, BLOCKS):
                if step == prepare_from[b]:
                    normalise(b)
                if step == prepare_from[b] + 1:
                    regroup(b)
                if step == prepare_from[b] + 2:
                    quantise_a(b)
            if step < 6:
                statistics(step + 2)
        for step in range(STEPS - LAG, STEPS):
            multiply(step)
